import numpy as np
import ml_dtypes


BF16 = ml_dtypes.bfloat16


def bf(x):
    return np.asarray(x, np.float32).astype(BF16)


def f64(x):
    return np.asarray(x).astype(np.float64)


E2M1 = np.array([0.0, 0.5, 1.0, 1.5, 2.0, 3.0, 4.0, 6.0, -0.0, -0.5, -1.0, -1.5, -2.0, -3.0, -4.0, -6.0])


def pack_weight(w, fmt):
    k, n = w.shape
    w = f64(bf(w)).reshape(k // 32, 32, n)
    amax = np.abs(w).max(1)
    if fmt == "e4m3":
        byte = np.frexp(amax)[1] - 1 + 127 - 7
    else:
        mant, ex = np.frexp(amax / 6.0)
        byte = np.where(mant > 0.5, ex, ex - 1) + 127
    byte = np.clip(np.where(amax > 0, byte, 1), 1, 254)
    scaled = (w * np.exp2(127.0 - byte)[:, None, :]).reshape(k, n).astype(np.float32)
    by_word = np.ascontiguousarray(scaled.reshape(k // 512, 128, 4, n).transpose(0, 1, 3, 2))
    if fmt == "e4m3":
        words = by_word.astype(ml_dtypes.float8_e4m3fn).view(np.uint8)
    else:
        c = by_word.astype(ml_dtypes.float4_e2m1fn).view(np.uint8) & 0xF
        words = c[..., 0::2] | (c[..., 1::2] << 4)
    return np.ascontiguousarray(words), np.ascontiguousarray(byte.astype(np.uint8).reshape(k // 512, 16, n))


def unpack_weight(words, scales, fmt):
    g, p, n, _ = words.shape
    if fmt == "e4m3":
        vals = np.ascontiguousarray(words).view(ml_dtypes.float8_e4m3fn).astype(np.float64)
    else:
        nib = np.empty((g, p, n, 4), np.uint8)
        nib[..., 0::2] = words & 0xF
        nib[..., 1::2] = words >> 4
        vals = E2M1[nib]
    vals = vals * np.repeat(np.exp2(scales.astype(np.float64) - 127.0), 8, axis=1)[..., None]
    return vals.transpose(0, 1, 3, 2).reshape(g * 512, n)

def pack4(w):
    words, scales = pack_weight(w, "e2m1")
    return words.reshape(words.shape[0], 128, -1), scales


def unpack4(words, scales):
    return unpack_weight(words.reshape(words.shape[0], 128, -1, 2), scales, "e2m1")


def kspread(k):
    return np.exp2(np.repeat(np.random.randint(-6, 7, k // 32), 32).astype(np.float64))


B, T, D, H, KVH, HD = 2, 512, 2048, 16, 4, 128
HALF = HD // 2
EPS = 1e-6
ROPE_BASE = 10000.0


def zc_rmsnorm(x, scale):
    rms = np.sqrt(np.mean(x ** 2, axis=-1, keepdims=True) + EPS)
    return (1.0 + scale) * x / rms


def apply_rope(x, cos, sin):
    t = x.shape[2]
    c = cos[:t][None, None, :, :]
    s = sin[:t][None, None, :, :]
    x1, x2 = x[..., :HALF], x[..., HALF:]
    return np.concatenate([x1 * c - x2 * s, x2 * c + x1 * s], axis=-1)


def setup_inputs():
    s = kspread(D)
    inv_freq = 1.0 / (ROPE_BASE ** (np.arange(0, HALF) / HALF))
    ang = np.arange(T)[:, None] * inv_freq[None, :]
    q_input = np.random.standard_normal((B, T, D)) * s
    q_input_words, q_input_scales = pack4(q_input.reshape(B * T, D).T)
    words, scales = pack4(np.random.standard_normal((D, H * HD)) / np.sqrt(D) / s[:, None])
    return {"q_input_words": q_input_words, "q_input_scales": q_input_scales,
            "Wq_words": words, "Wq_scales": scales,
            "q_scale": bf(np.random.standard_normal(HD) * 0.2),
            "cos": bf(np.cos(ang)), "sin": bf(np.sin(ang))}


def reference(q_input_words, q_input_scales, Wq_words, Wq_scales, q_scale, cos, sin):
    b = B
    q = unpack4(q_input_words, q_input_scales).T.reshape(B, T, D) @ unpack4(Wq_words, Wq_scales)
    q = q.reshape(b, -1, H, HD).transpose(0, 2, 1, 3)
    q = zc_rmsnorm(q, f64(q_scale))
    return apply_rope(q, f64(cos), f64(sin))

@@ -1,0 +1,201 @@
+from contextlib import ExitStack
+
+import concourse.mybir as mybir
+
+F32 = mybir.dt.float32
+BF16 = mybir.dt.bfloat16
+U8 = mybir.dt.uint8
+I32 = mybir.dt.int32
+FP4X4 = mybir.dt.float4_e2m1fn_x4
+ACT = mybir.ActivationFunctionType
+ALU = mybir.AluOpType
+
+B, T, D, H, HD = 2, 512, 2048, 16, 128
+HALF = HD // 2
+EPS = 1e-6
+P = 128
+PASSES = D // 512
+N_TILE = 512
+HEADS_PER_BANK = N_TILE // HD
+M_TILES = B * T // P
+POS_BLOCKS = T // P
+FLOPS = 2 * B * T * D * H * HD
+
+N_WARM = 8
+X_CHUNKS = ((0, 256), (256, 1024))
+
+
+def tile_multiheadattention_pa_kernel(
+    tc, q_input_words, q_input_scales, Wq_words, Wq_scales, q_scale, cos, sin, out
+):
+    nc = tc.nc
+    with ExitStack() as ctx:
+        const = ctx.enter_context(tc.tile_pool(name="const", bufs=1))
+        stats = ctx.enter_context(tc.tile_pool(name="stats", bufs=6))
+        work = ctx.enter_context(tc.tile_pool(name="work", bufs=4))
+        psum = ctx.enter_context(tc.psum_pool(name="psum", bufs=8))
+
+        xc = []
+        xs = []
+        for i, (t0, t1) in enumerate(X_CHUNKS):
+            xc_t = const.tile([P, PASSES, 2 * (t1 - t0)], U8, name="xc%d" % i, align_bytes=64)
+            xs_t = const.tile([P, PASSES, t1 - t0], U8, name="xs%d" % i, align_bytes=64)
+            xc.append(xc_t)
+            xs.append(xs_t)
+        wc = []
+        ws = []
+        for n in range(4):
+            wc_t = const.tile([P, PASSES, 2 * N_TILE], U8, name="wc%d" % n, align_bytes=64)
+            ws_t = const.tile([P, PASSES, N_TILE], U8, name="ws%d" % n, align_bytes=64)
+            wc.append(wc_t)
+            ws.append(ws_t)
+
+        eps_t = const.tile([P, 1], F32, name="eps_t")
+        scr_t = const.tile([P, 1], F32, name="scr_t")
+        ones = const.tile([P, N_TILE], BF16, name="ones")
+        qrow = const.tile([P, 256], BF16, name="qrow")
+        cos_sb = const.tile([P, POS_BLOCKS, HALF], BF16, name="cos_sb")
+        sin_sb = const.tile([P, POS_BLOCKS, HALF], BF16, name="sin_sb")
+        gpos = const.tile([P, HD], F32, name="gpos")
+        gneg = const.tile([P, HALF], F32, name="gneg")
+        tab_a = const.tile([P, POS_BLOCKS, HD], F32, name="tab_a")
+        tab_b = const.tile([P, POS_BLOCKS, HD], F32, name="tab_b")
+
+        def zero_plane(t):
+            nc.vector.memset(t[:].rearrange("p g c -> p (g c)").bitcast(I32), 0)
+
+        def load_codes(dst, src, b0, b1):
+            nc.sync.dma_start(
+                out=dst[:].bitcast(I32),
+                in_=src[:, :, b0:b1].rearrange("g p c -> p g c").bitcast(I32),
+            )
+
+        def load_scales(dst, src, c0, c1, quads):
+            for q in quads:
+                nc.sync.dma_start(
+                    out=dst[32 * q : 32 * q + 4, :, :].bitcast(I32),
+                    in_=src[:, 4 * q : 4 * q + 4, c0:c1].rearrange("g r c -> r g c").bitcast(I32),
+                )
+
+        nc.vector.memset(eps_t[:], EPS)
+        zero_plane(xs[0])
+        zero_plane(ws[0])
+        zero_plane(ws[1])
+        zero_plane(xs[1])
+        zero_plane(ws[2])
+        zero_plane(ws[3])
+
+        nc.gpsimd.memset(qrow[:], 0.0)
+        nc.gpsimd.dma_start(out=qrow[0:1, 0:HD], in_=q_scale.rearrange("(o n) -> o n", o=1))
+        nc.gpsimd.memset(ones[:], 1.0)
+        nc.gpsimd.dma_start(out=cos_sb[:], in_=cos.rearrange("(a p) j -> p a j", p=P))
+        nc.gpsimd.dma_start(out=sin_sb[:], in_=sin.rearrange("(a p) j -> p a j", p=P))
+
+        nc.scalar.activation(out=scr_t[:], in_=eps_t[:], func=ACT.Abs_reciprocal_sqrt)
+
+        load_scales(xs[0], q_input_scales, 0, 256, (0, 1))
+        load_codes(xc[0], q_input_words, 0, 512)
+        load_codes(wc[0], Wq_words, 0, 1024)
+        load_scales(xs[0], q_input_scales, 0, 256, (2, 3))
+        load_scales(ws[0], Wq_scales, 0, 512, (0, 1, 2, 3))
+        load_scales(ws[1], Wq_scales, 512, 1024, (0, 1, 2, 3))
+        load_codes(wc[1], Wq_words, 1024, 2048)
+        load_codes(xc[1], q_input_words, 512, 2048)
+        load_scales(xs[1], q_input_scales, 256, 1024, (0, 1, 2, 3))
+        load_scales(ws[2], Wq_scales, 1024, 1536, (0, 1, 2, 3))
+        load_codes(wc[2], Wq_words, 2048, 3072)
+        load_scales(ws[3], Wq_scales, 1536, 2048, (0, 1, 2, 3))
+        load_codes(wc[3], Wq_words, 3072, 4096)
+
+        warm_ps = psum.tile([P, N_TILE], F32, name="warm_ps", tag="acc")
+        for k in range(N_WARM):
+            nc.tensor.matmul(out=warm_ps[:], lhsT=ones[:, 0:P], rhs=ones[:], start=True, stop=True)
+        q_ps = psum.tile([P, N_TILE], F32, name="q_ps", tag="acc")
+        nc.tensor.matmul(out=q_ps[:, 0:256], lhsT=ones[:, 0:P], rhs=qrow[:], start=True, stop=True)
+
+        nc.vector.tensor_scalar(out=gpos[:], in0=q_ps[:, 0:HD], scalar1=1.0, scalar2=None, op0=ALU.add)
+        nc.vector.tensor_scalar(
+            out=gneg[:], in0=q_ps[:, HALF:HD], scalar1=-1.0, scalar2=-1.0, op0=ALU.mult, op1=ALU.add
+        )
+        for a in range(POS_BLOCKS):
+            nc.vector.tensor_tensor(out=tab_a[:, a, 0:HALF], in0=gpos[:, 0:HALF], in1=cos_sb[:, a, :], op=ALU.mult)
+            nc.vector.tensor_tensor(out=tab_a[:, a, HALF:HD], in0=gpos[:, HALF:HD], in1=cos_sb[:, a, :], op=ALU.mult)
+            nc.vector.tensor_tensor(out=tab_b[:, a, 0:HALF], in0=gneg[:], in1=sin_sb[:, a, :], op=ALU.mult)
+            nc.vector.tensor_tensor(out=tab_b[:, a, HALF:HD], in0=gpos[:, 0:HALF], in1=sin_sb[:, a, :], op=ALU.mult)
+
+        def x_slices(m, g):
+            t0 = P * m
+            for i, (c0, c1) in enumerate(X_CHUNKS):
+                if c0 <= t0 < c1:
+                    o = t0 - c0
+                    return xc[i][:, g, 2 * o : 2 * o + 2 * P], xs[i][:, g, o : o + P]
+            raise ValueError("token tile outside the chunks")
+
+        order = [(0, 0), (1, 0), (0, 1), (1, 1)]
+        for m in range(2, M_TILES):
+            order.extend([(m, 0), (m, 1)])
+        for m in range(M_TILES):
+            order.extend([(m, 2), (m, 3)])
+
+        pair_tiles = {}
+        for m, n in order:
+            pb = m % POS_BLOCKS
+            b = m // POS_BLOCKS
+            acc = psum.tile([P, N_TILE], F32, name="acc", tag="acc")
+            for g in range(PASSES):
+                x_codes, x_scales = x_slices(m, g)
+                nc.tensor.matmul_mx(
+                    out=acc[:],
+                    lhsT=x_codes.bitcast(FP4X4),
+                    lhsT_scale=x_scales,
+                    rhs=wc[n][:, g, :].bitcast(FP4X4),
+                    rhs_scale=ws[n][:, g, :],
+                    start=(g == 0),
+                    stop=(g == PASSES - 1),
+                )
+
+            ss = stats.tile([P, HEADS_PER_BANK], F32, name="ss")
+            rstd = stats.tile([P, HEADS_PER_BANK], F32, name="rstd")
+            for h in range(HEADS_PER_BANK):
+                junk = stats.tile([P, HD], BF16, name="junk")
+                nc.scalar.activation(
+                    out=junk[:], in_=acc[:, HD * h : HD * (h + 1)], func=ACT.Square, accum_out=ss[:, h : h + 1]
+                )
+            nc.scalar.activation(
+                out=rstd[:], in_=ss[:], func=ACT.Abs_reciprocal_sqrt, bias=eps_t[:, 0:1], scale=1.0 / HD
+            )
+
+            key = (m, n // 2)
+            if key not in pair_tiles:
+                u_t = work.tile([P, 2 * N_TILE], F32, name="u_t")
+                w_t = work.tile([P, 2 * N_TILE], F32, name="w_t")
+                pair_tiles[key] = (u_t, w_t, [])
+            u_t, w_t, done = pair_tiles[key]
+            for h in range(HEADS_PER_BANK):
+                c0 = N_TILE * (n % 2) + HD * h
+                a_h = acc[:, HD * h : HD * (h + 1)]
+                nc.vector.scalar_tensor_tensor(
+                    out=u_t[:, c0 : c0 + HD],
+                    in0=a_h,
+                    scalar=rstd[:, h : h + 1],
+                    in1=tab_a[:, pb, :],
+                    op0=ALU.mult,
+                    op1=ALU.mult,
+                )
+                nc.vector.scalar_tensor_tensor(
+                    out=w_t[:, c0 : c0 + HD].rearrange("p (t j) -> p t j", t=2),
+                    in0=a_h.rearrange("p (t j) -> p t j", t=2)[:, ::-1, :],
+                    scalar=rstd[:, h : h + 1],
+                    in1=tab_b[:, pb, :].rearrange("p (t j) -> p t j", t=2),
+                    op0=ALU.mult,
+                    op1=ALU.mult,
+                )
+            done.append(n)
+            if len(done) == 2:
+                z_t = work.tile([P, 2 * N_TILE], F32, name="z_t")
+                nc.gpsimd.tensor_tensor(out=z_t[:], in0=u_t[:], in1=w_t[:], op=ALU.add)
+                h0 = 2 * HEADS_PER_BANK * (n // 2)
+                nc.sync.dma_start(
+                    out=out[b, h0 : h0 + 2 * HEADS_PER_BANK, P * pb : P * (pb + 1), :].rearrange("h p d -> p h d"),
+                    in_=z_t[:].rearrange("p (h d) -> p h d", d=HD),
+                )

@@ -21,7 +21,7 @@ M_TILES = B * T // P
 POS_BLOCKS = T // P
 FLOPS = 2 * B * T * D * H * HD
 
-N_WARM = 8
+N_WARM = 10
 X_CHUNKS = ((0, 256), (256, 1024))
 
 
@@ -137,10 +137,50 @@ def tile_multiheadattention_pa_kernel(
         for m in range(M_TILES):
             order.extend([(m, 2), (m, 3)])
 
-        pair_tiles = {}
-        for m, n in order:
-            pb = m % POS_BLOCKS
+        jobs = [("g", 0, 1), ("g", 1, 1)]
+        for i in range(2, 28, 2):
+            jobs.append(("g", i, 2))
+        jobs.extend([("g", 28, 1), ("v", 29, 1), ("v", 30, 1), ("v", 31, 1)])
+        job_of = {}
+        for j, (eng, first, count) in enumerate(jobs):
+            for i in range(first, first + count):
+                job_of[i] = j
+        job_tiles = {}
+        late_adds = []
+
+        def store(z_ap, m, h0, heads):
             b = m // POS_BLOCKS
+            pb = m % POS_BLOCKS
+            nc.sync.dma_start(
+                out=out[b, h0 : h0 + heads, P * pb : P * (pb + 1), :].rearrange("h p d -> p h d"),
+                in_=z_ap.rearrange("p (h d) -> p h d", d=HD),
+            )
+
+        def add_and_store(j):
+            eng, first, count = jobs[j]
+            u_t, w_t = job_tiles[j]
+            width = N_TILE * count
+            z_t = work.tile([P, width], F32, name="z_t", bufs=8)
+            if eng == "g":
+                nc.gpsimd.tensor_tensor(out=z_t[:], in0=u_t[:], in1=w_t[:], op=ALU.add)
+                m0, n0 = order[first]
+                if count == 2 and order[first + 1] == (m0, n0 + 1):
+                    store(z_t[:], m0, HEADS_PER_BANK * n0, 2 * HEADS_PER_BANK)
+                else:
+                    for s in range(count):
+                        ms, ns = order[first + s]
+                        store(z_t[:, N_TILE * s : N_TILE * (s + 1)], ms, HEADS_PER_BANK * ns, HEADS_PER_BANK)
+            else:
+                m0, n0 = order[first]
+                pieces = 2 if first == len(order) - 1 else 1
+                wp = width // pieces
+                for s in range(pieces):
+                    cs = slice(wp * s, wp * (s + 1))
+                    nc.vector.tensor_tensor(out=z_t[:, cs], in0=u_t[:, cs], in1=w_t[:, cs], op=ALU.add)
+                    store(z_t[:, cs], m0, HEADS_PER_BANK * n0 + (wp // HD) * s, wp // HD)
+
+        for i, (m, n) in enumerate(order):
+            pb = m % POS_BLOCKS
             acc = psum.tile([P, N_TILE], F32, name="acc", tag="acc")
             for g in range(PASSES):
                 x_codes, x_scales = x_slices(m, g)
@@ -165,14 +205,15 @@ def tile_multiheadattention_pa_kernel(
                 out=rstd[:], in_=ss[:], func=ACT.Abs_reciprocal_sqrt, bias=eps_t[:, 0:1], scale=1.0 / HD
             )
 
-            key = (m, n // 2)
-            if key not in pair_tiles:
-                u_t = work.tile([P, 2 * N_TILE], F32, name="u_t")
-                w_t = work.tile([P, 2 * N_TILE], F32, name="w_t")
-                pair_tiles[key] = (u_t, w_t, [])
-            u_t, w_t, done = pair_tiles[key]
+            j = job_of[i]
+            eng, first, count = jobs[j]
+            if i == first:
+                u_new = work.tile([P, N_TILE * count], F32, name="u_t", bufs=6)
+                w_new = work.tile([P, N_TILE * count], F32, name="w_t", bufs=6)
+                job_tiles[j] = (u_new, w_new)
+            u_t, w_t = job_tiles[j]
             for h in range(HEADS_PER_BANK):
-                c0 = N_TILE * (n % 2) + HD * h
+                c0 = N_TILE * (i - first) + HD * h
                 a_h = acc[:, HD * h : HD * (h + 1)]
                 nc.vector.scalar_tensor_tensor(
                     out=u_t[:, c0 : c0 + HD],
@@ -190,12 +231,10 @@ def tile_multiheadattention_pa_kernel(
                     op0=ALU.mult,
                     op1=ALU.mult,
                 )
-            done.append(n)
-            if len(done) == 2:
-                z_t = work.tile([P, 2 * N_TILE], F32, name="z_t")
-                nc.gpsimd.tensor_tensor(out=z_t[:], in0=u_t[:], in1=w_t[:], op=ALU.add)
-                h0 = 2 * HEADS_PER_BANK * (n // 2)
-                nc.sync.dma_start(
-                    out=out[b, h0 : h0 + 2 * HEADS_PER_BANK, P * pb : P * (pb + 1), :].rearrange("h p d -> p h d"),
-                    in_=z_t[:].rearrange("p (h d) -> p h d", d=HD),
-                )
+            if i == first + count - 1:
+                if eng == "g":
+                    add_and_store(j)
+                else:
+                    late_adds.append(j)
+        for j in late_adds:
+            add_and_store(j)

@@ -58,8 +58,7 @@ def tile_multiheadattention_pa_kernel(
         sin_sb = const.tile([P, POS_BLOCKS, HALF], BF16, name="sin_sb")
         gpos = const.tile([P, HD], F32, name="gpos")
         gneg = const.tile([P, HALF], F32, name="gneg")
-        tab_a = const.tile([P, POS_BLOCKS, HD], F32, name="tab_a")
-        tab_b = const.tile([P, POS_BLOCKS, HD], F32, name="tab_b")
+        tab = const.tile([P, POS_BLOCKS, 2 * HD], F32, name="tab")
 
         def zero_plane(t):
             nc.vector.memset(t[:].rearrange("p g c -> p (g c)").bitcast(I32), 0)
@@ -118,10 +117,10 @@ def tile_multiheadattention_pa_kernel(
             out=gneg[:], in0=q_ps[:, HALF:HD], scalar1=-1.0, scalar2=-1.0, op0=ALU.mult, op1=ALU.add
         )
         for a in range(POS_BLOCKS):
-            nc.vector.tensor_tensor(out=tab_a[:, a, 0:HALF], in0=gpos[:, 0:HALF], in1=cos_sb[:, a, :], op=ALU.mult)
-            nc.vector.tensor_tensor(out=tab_a[:, a, HALF:HD], in0=gpos[:, HALF:HD], in1=cos_sb[:, a, :], op=ALU.mult)
-            nc.vector.tensor_tensor(out=tab_b[:, a, 0:HALF], in0=gneg[:], in1=sin_sb[:, a, :], op=ALU.mult)
-            nc.vector.tensor_tensor(out=tab_b[:, a, HALF:HD], in0=gpos[:, 0:HALF], in1=sin_sb[:, a, :], op=ALU.mult)
+            nc.vector.tensor_tensor(out=tab[:, a, 0:HALF], in0=gpos[:, 0:HALF], in1=cos_sb[:, a, :], op=ALU.mult)
+            nc.vector.tensor_tensor(out=tab[:, a, HALF:HD], in0=gneg[:], in1=sin_sb[:, a, :], op=ALU.mult)
+            nc.vector.tensor_tensor(out=tab[:, a, HD : HD + HALF], in0=gpos[:, 0:HALF], in1=sin_sb[:, a, :], op=ALU.mult)
+            nc.vector.tensor_tensor(out=tab[:, a, HD + HALF : 2 * HD], in0=gpos[:, HALF:HD], in1=cos_sb[:, a, :], op=ALU.mult)
 
         def x_slices(m, g):
             t0 = P * m
@@ -158,11 +157,13 @@ def tile_multiheadattention_pa_kernel(
 
         def add_and_store(j):
             eng, first, count = jobs[j]
-            u_t, w_t = job_tiles[j]
+            p_t = job_tiles[j]
             width = N_TILE * count
             z_t = work.tile([P, width], F32, name="z_t", bufs=8)
+            p_v = p_t[:].rearrange("p (n b j) -> p n b j", b=2, j=HALF)
+            z_v = z_t[:].rearrange("p (n j) -> p n j", j=HALF)
             if eng == "g":
-                nc.gpsimd.tensor_tensor(out=z_t[:], in0=u_t[:], in1=w_t[:], op=ALU.add)
+                nc.gpsimd.tensor_tensor(out=z_v, in0=p_v[:, :, 0, :], in1=p_v[:, :, 1, :], op=ALU.add)
                 m0, n0 = order[first]
                 if count == 2 and order[first + 1] == (m0, n0 + 1):
                     store(z_t[:], m0, HEADS_PER_BANK * n0, 2 * HEADS_PER_BANK)
@@ -176,7 +177,8 @@ def tile_multiheadattention_pa_kernel(
                 wp = width // pieces
                 for s in range(pieces):
                     cs = slice(wp * s, wp * (s + 1))
-                    nc.vector.tensor_tensor(out=z_t[:, cs], in0=u_t[:, cs], in1=w_t[:, cs], op=ALU.add)
+                    ns = slice(wp // HALF * s, wp // HALF * (s + 1))
+                    nc.vector.tensor_tensor(out=z_v[:, ns, :], in0=p_v[:, ns, 0, :], in1=p_v[:, ns, 1, :], op=ALU.add)
                     store(z_t[:, cs], m0, HEADS_PER_BANK * n0 + (wp // HD) * s, wp // HD)
 
         for i, (m, n) in enumerate(order):
@@ -208,26 +210,17 @@ def tile_multiheadattention_pa_kernel(
             j = job_of[i]
             eng, first, count = jobs[j]
             if i == first:
-                u_new = work.tile([P, N_TILE * count], F32, name="u_t", bufs=6)
-                w_new = work.tile([P, N_TILE * count], F32, name="w_t", bufs=6)
-                job_tiles[j] = (u_new, w_new)
-            u_t, w_t = job_tiles[j]
+                p_new = work.tile([P, 2 * N_TILE * count], F32, name="p_t", bufs=6)
+                job_tiles[j] = p_new
+            p_t = job_tiles[j]
             for h in range(HEADS_PER_BANK):
-                c0 = N_TILE * (i - first) + HD * h
+                c0 = 2 * (N_TILE * (i - first) + HD * h)
                 a_h = acc[:, HD * h : HD * (h + 1)]
                 nc.vector.scalar_tensor_tensor(
-                    out=u_t[:, c0 : c0 + HD],
-                    in0=a_h,
+                    out=p_t[:, c0 : c0 + 2 * HD].rearrange("p (a b j) -> p a b j", a=2, b=2),
+                    in0=a_h.rearrange("p (b j) -> p b j", b=2).unsqueeze(1).to_broadcast([P, 2, 2, HALF]),
                     scalar=rstd[:, h : h + 1],
-                    in1=tab_a[:, pb, :],
-                    op0=ALU.mult,
-                    op1=ALU.mult,
-                )
-                nc.vector.scalar_tensor_tensor(
-                    out=w_t[:, c0 : c0 + HD].rearrange("p (t j) -> p t j", t=2),
-                    in0=a_h.rearrange("p (t j) -> p t j", t=2)[:, ::-1, :],
-                    scalar=rstd[:, h : h + 1],
-                    in1=tab_b[:, pb, :].rearrange("p (t j) -> p t j", t=2),
+                    in1=tab[:, pb, :].rearrange("p (a b j) -> p a b j", a=2, b=2),
                     op0=ALU.mult,
                     op1=ALU.mult,
                 )

@@ -76,6 +76,11 @@ def tile_multiheadattention_pa_kernel(
                     in_=src[:, 4 * q : 4 * q + 4, c0:c1].rearrange("g r c -> r g c").bitcast(I32),
                 )
 
+        nc.vector.memset(qrow[:], 0.0)
+        nc.scalar.dma_start(out=qrow[0:1, 0:HD], in_=q_scale.rearrange("(o n) -> o n", o=1))
+        nc.gpsimd.memset(ones[:], 1.0)
+        nc.gpsimd.dma_start(out=cos_sb[:], in_=cos.rearrange("(a p) j -> p a j", p=P))
+        nc.gpsimd.dma_start(out=sin_sb[:], in_=sin.rearrange("(a p) j -> p a j", p=P))
         nc.vector.memset(eps_t[:], EPS)
         zero_plane(xs[0])
         zero_plane(ws[0])
@@ -83,12 +88,6 @@ def tile_multiheadattention_pa_kernel(
         zero_plane(xs[1])
         zero_plane(ws[2])
         zero_plane(ws[3])
-
-        nc.gpsimd.memset(qrow[:], 0.0)
-        nc.gpsimd.dma_start(out=qrow[0:1, 0:HD], in_=q_scale.rearrange("(o n) -> o n", o=1))
-        nc.gpsimd.memset(ones[:], 1.0)
-        nc.gpsimd.dma_start(out=cos_sb[:], in_=cos.rearrange("(a p) j -> p a j", p=P))
-        nc.gpsimd.dma_start(out=sin_sb[:], in_=sin.rearrange("(a p) j -> p a j", p=P))
 
         nc.scalar.activation(out=scr_t[:], in_=eps_t[:], func=ACT.Abs_reciprocal_sqrt)
 
@@ -118,9 +117,10 @@ def tile_multiheadattention_pa_kernel(
         )
         for a in range(POS_BLOCKS):
             nc.vector.tensor_tensor(out=tab[:, a, 0:HALF], in0=gpos[:, 0:HALF], in1=cos_sb[:, a, :], op=ALU.mult)
+            nc.vector.tensor_tensor(out=tab[:, a, HD + HALF : 2 * HD], in0=gpos[:, HALF:HD], in1=cos_sb[:, a, :], op=ALU.mult)
+        for a in range(POS_BLOCKS):
             nc.vector.tensor_tensor(out=tab[:, a, HALF:HD], in0=gneg[:], in1=sin_sb[:, a, :], op=ALU.mult)
             nc.vector.tensor_tensor(out=tab[:, a, HD : HD + HALF], in0=gpos[:, 0:HALF], in1=sin_sb[:, a, :], op=ALU.mult)
-            nc.vector.tensor_tensor(out=tab[:, a, HD + HALF : 2 * HD], in0=gpos[:, HALF:HD], in1=cos_sb[:, a, :], op=ALU.mult)
 
         def x_slices(m, g):
             t0 = P * m

@@ -21,7 +21,7 @@ M_TILES = B * T // P
 POS_BLOCKS = T // P
 FLOPS = 2 * B * T * D * H * HD
 
-N_WARM = 10
+N_WARM = 15
 X_CHUNKS = ((0, 256), (256, 1024))
 
 

from contextlib import ExitStack

import concourse.mybir as mybir

F32 = mybir.dt.float32
BF16 = mybir.dt.bfloat16
U8 = mybir.dt.uint8
I32 = mybir.dt.int32
FP4X4 = mybir.dt.float4_e2m1fn_x4
ACT = mybir.ActivationFunctionType
ALU = mybir.AluOpType

B, T, D, H, HD = 2, 512, 2048, 16, 128
HALF = HD // 2
EPS = 1e-6
P = 128
PASSES = D // 512
N_TILE = 512
HEADS_PER_BANK = N_TILE // HD
M_TILES = B * T // P
POS_BLOCKS = T // P
FLOPS = 2 * B * T * D * H * HD

N_WARM = 15
X_CHUNKS = ((0, 256), (256, 1024))


def tile_multiheadattention_pa_kernel(
    tc, q_input_words, q_input_scales, Wq_words, Wq_scales, q_scale, cos, sin, out
):
    nc = tc.nc
    with ExitStack() as ctx:
        const = ctx.enter_context(tc.tile_pool(name="const", bufs=1))
        stats = ctx.enter_context(tc.tile_pool(name="stats", bufs=6))
        work = ctx.enter_context(tc.tile_pool(name="work", bufs=4))
        psum = ctx.enter_context(tc.psum_pool(name="psum", bufs=8))

        xc = []
        xs = []
        for i, (t0, t1) in enumerate(X_CHUNKS):
            xc_t = const.tile([P, PASSES, 2 * (t1 - t0)], U8, name="xc%d" % i, align_bytes=64)
            xs_t = const.tile([P, PASSES, t1 - t0], U8, name="xs%d" % i, align_bytes=64)
            xc.append(xc_t)
            xs.append(xs_t)
        wc = []
        ws = []
        for n in range(4):
            wc_t = const.tile([P, PASSES, 2 * N_TILE], U8, name="wc%d" % n, align_bytes=64)
            ws_t = const.tile([P, PASSES, N_TILE], U8, name="ws%d" % n, align_bytes=64)
            wc.append(wc_t)
            ws.append(ws_t)

        eps_t = const.tile([P, 1], F32, name="eps_t")
        scr_t = const.tile([P, 1], F32, name="scr_t")
        ones = const.tile([P, N_TILE], BF16, name="ones")
        qrow = const.tile([P, 256], BF16, name="qrow")
        cos_sb = const.tile([P, POS_BLOCKS, HALF], BF16, name="cos_sb")
        sin_sb = const.tile([P, POS_BLOCKS, HALF], BF16, name="sin_sb")
        gpos = const.tile([P, HD], F32, name="gpos")
        gneg = const.tile([P, HALF], F32, name="gneg")
        tab = const.tile([P, POS_BLOCKS, 2 * HD], F32, name="tab")

        def zero_plane(t):
            nc.vector.memset(t[:].rearrange("p g c -> p (g c)").bitcast(I32), 0)

        def load_codes(dst, src, b0, b1):
            nc.sync.dma_start(
                out=dst[:].bitcast(I32),
                in_=src[:, :, b0:b1].rearrange("g p c -> p g c").bitcast(I32),
            )

        def load_scales(dst, src, c0, c1, quads):
            for q in quads:
                nc.sync.dma_start(
                    out=dst[32 * q : 32 * q + 4, :, :].bitcast(I32),
                    in_=src[:, 4 * q : 4 * q + 4, c0:c1].rearrange("g r c -> r g c").bitcast(I32),
                )

        nc.vector.memset(qrow[:], 0.0)
        nc.scalar.dma_start(out=qrow[0:1, 0:HD], in_=q_scale.rearrange("(o n) -> o n", o=1))
        nc.gpsimd.memset(ones[:], 1.0)
        nc.gpsimd.dma_start(out=cos_sb[:], in_=cos.rearrange("(a p) j -> p a j", p=P))
        nc.gpsimd.dma_start(out=sin_sb[:], in_=sin.rearrange("(a p) j -> p a j", p=P))
        nc.vector.memset(eps_t[:], EPS)
        zero_plane(xs[0])
        zero_plane(ws[0])
        zero_plane(ws[1])
        zero_plane(xs[1])
        zero_plane(ws[2])
        zero_plane(ws[3])

        nc.scalar.activation(out=scr_t[:], in_=eps_t[:], func=ACT.Abs_reciprocal_sqrt)

        load_scales(xs[0], q_input_scales, 0, 256, (0, 1))
        load_codes(xc[0], q_input_words, 0, 512)
        load_codes(wc[0], Wq_words, 0, 1024)
        load_scales(xs[0], q_input_scales, 0, 256, (2, 3))
        load_scales(ws[0], Wq_scales, 0, 512, (0, 1, 2, 3))
        load_scales(ws[1], Wq_scales, 512, 1024, (0, 1, 2, 3))
        load_codes(wc[1], Wq_words, 1024, 2048)
        load_codes(xc[1], q_input_words, 512, 2048)
        load_scales(xs[1], q_input_scales, 256, 1024, (0, 1, 2, 3))
        load_scales(ws[2], Wq_scales, 1024, 1536, (0, 1, 2, 3))
        load_codes(wc[2], Wq_words, 2048, 3072)
        load_scales(ws[3], Wq_scales, 1536, 2048, (0, 1, 2, 3))
        load_codes(wc[3], Wq_words, 3072, 4096)

        warm_ps = psum.tile([P, N_TILE], F32, name="warm_ps", tag="acc")
        for k in range(N_WARM):
            nc.tensor.matmul(out=warm_ps[:], lhsT=ones[:, 0:P], rhs=ones[:], start=True, stop=True)
        q_ps = psum.tile([P, N_TILE], F32, name="q_ps", tag="acc")
        nc.tensor.matmul(out=q_ps[:, 0:256], lhsT=ones[:, 0:P], rhs=qrow[:], start=True, stop=True)

        nc.vector.tensor_scalar(out=gpos[:], in0=q_ps[:, 0:HD], scalar1=1.0, scalar2=None, op0=ALU.add)
        nc.vector.tensor_scalar(
            out=gneg[:], in0=q_ps[:, HALF:HD], scalar1=-1.0, scalar2=-1.0, op0=ALU.mult, op1=ALU.add
        )
        for a in range(POS_BLOCKS):
            nc.vector.tensor_tensor(out=tab[:, a, 0:HALF], in0=gpos[:, 0:HALF], in1=cos_sb[:, a, :], op=ALU.mult)
            nc.vector.tensor_tensor(out=tab[:, a, HD + HALF : 2 * HD], in0=gpos[:, HALF:HD], in1=cos_sb[:, a, :], op=ALU.mult)
        for a in range(POS_BLOCKS):
            nc.vector.tensor_tensor(out=tab[:, a, HALF:HD], in0=gneg[:], in1=sin_sb[:, a, :], op=ALU.mult)
            nc.vector.tensor_tensor(out=tab[:, a, HD : HD + HALF], in0=gpos[:, 0:HALF], in1=sin_sb[:, a, :], op=ALU.mult)

        def x_slices(m, g):
            t0 = P * m
            for i, (c0, c1) in enumerate(X_CHUNKS):
                if c0 <= t0 < c1:
                    o = t0 - c0
                    return xc[i][:, g, 2 * o : 2 * o + 2 * P], xs[i][:, g, o : o + P]
            raise ValueError("token tile outside the chunks")

        order = [(0, 0), (1, 0), (0, 1), (1, 1)]
        for m in range(2, M_TILES):
            order.extend([(m, 0), (m, 1)])
        for m in range(M_TILES):
            order.extend([(m, 2), (m, 3)])

        jobs = [("g", 0, 1), ("g", 1, 1)]
        for i in range(2, 28, 2):
            jobs.append(("g", i, 2))
        jobs.extend([("g", 28, 1), ("v", 29, 1), ("v", 30, 1), ("v", 31, 1)])
        job_of = {}
        for j, (eng, first, count) in enumerate(jobs):
            for i in range(first, first + count):
                job_of[i] = j
        job_tiles = {}
        late_adds = []

        def store(z_ap, m, h0, heads):
            b = m // POS_BLOCKS
            pb = m % POS_BLOCKS
            nc.sync.dma_start(
                out=out[b, h0 : h0 + heads, P * pb : P * (pb + 1), :].rearrange("h p d -> p h d"),
                in_=z_ap.rearrange("p (h d) -> p h d", d=HD),
            )

        def add_and_store(j):
            eng, first, count = jobs[j]
            p_t = job_tiles[j]
            width = N_TILE * count
            z_t = work.tile([P, width], F32, name="z_t", bufs=8)
            p_v = p_t[:].rearrange("p (n b j) -> p n b j", b=2, j=HALF)
            z_v = z_t[:].rearrange("p (n j) -> p n j", j=HALF)
            if eng == "g":
                nc.gpsimd.tensor_tensor(out=z_v, in0=p_v[:, :, 0, :], in1=p_v[:, :, 1, :], op=ALU.add)
                m0, n0 = order[first]
                if count == 2 and order[first + 1] == (m0, n0 + 1):
                    store(z_t[:], m0, HEADS_PER_BANK * n0, 2 * HEADS_PER_BANK)
                else:
                    for s in range(count):
                        ms, ns = order[first + s]
                        store(z_t[:, N_TILE * s : N_TILE * (s + 1)], ms, HEADS_PER_BANK * ns, HEADS_PER_BANK)
            else:
                m0, n0 = order[first]
                pieces = 2 if first == len(order) - 1 else 1
                wp = width // pieces
                for s in range(pieces):
                    cs = slice(wp * s, wp * (s + 1))
                    ns = slice(wp // HALF * s, wp // HALF * (s + 1))
                    nc.vector.tensor_tensor(out=z_v[:, ns, :], in0=p_v[:, ns, 0, :], in1=p_v[:, ns, 1, :], op=ALU.add)
                    store(z_t[:, cs], m0, HEADS_PER_BANK * n0 + (wp // HD) * s, wp // HD)

        for i, (m, n) in enumerate(order):
            pb = m % POS_BLOCKS
            acc = psum.tile([P, N_TILE], F32, name="acc", tag="acc")
            for g in range(PASSES):
                x_codes, x_scales = x_slices(m, g)
                nc.tensor.matmul_mx(
                    out=acc[:],
                    lhsT=x_codes.bitcast(FP4X4),
                    lhsT_scale=x_scales,
                    rhs=wc[n][:, g, :].bitcast(FP4X4),
                    rhs_scale=ws[n][:, g, :],
                    start=(g == 0),
                    stop=(g == PASSES - 1),
                )

            ss = stats.tile([P, HEADS_PER_BANK], F32, name="ss")
            rstd = stats.tile([P, HEADS_PER_BANK], F32, name="rstd")
            for h in range(HEADS_PER_BANK):
                junk = stats.tile([P, HD], BF16, name="junk")
                nc.scalar.activation(
                    out=junk[:], in_=acc[:, HD * h : HD * (h + 1)], func=ACT.Square, accum_out=ss[:, h : h + 1]
                )
            nc.scalar.activation(
                out=rstd[:], in_=ss[:], func=ACT.Abs_reciprocal_sqrt, bias=eps_t[:, 0:1], scale=1.0 / HD
            )

            j = job_of[i]
            eng, first, count = jobs[j]
            if i == first:
                p_new = work.tile([P, 2 * N_TILE * count], F32, name="p_t", bufs=6)
                job_tiles[j] = p_new
            p_t = job_tiles[j]
            for h in range(HEADS_PER_BANK):
                c0 = 2 * (N_TILE * (i - first) + HD * h)
                a_h = acc[:, HD * h : HD * (h + 1)]
                nc.vector.scalar_tensor_tensor(
                    out=p_t[:, c0 : c0 + 2 * HD].rearrange("p (a b j) -> p a b j", a=2, b=2),
                    in0=a_h.rearrange("p (b j) -> p b j", b=2).unsqueeze(1).to_broadcast([P, 2, 2, HALF]),
                    scalar=rstd[:, h : h + 1],
                    in1=tab[:, pb, :].rearrange("p (a b j) -> p a b j", a=2, b=2),
                    op0=ALU.mult,
                    op1=ALU.mult,
                )
            if i == first + count - 1:
                if eng == "g":
                    add_and_store(j)
                else:
                    late_adds.append(j)
        for j in late_adds:
            add_and_store(j)
